import numpy as np
import ml_dtypes


def mxq(x, axis, fmt="e4m3"):
    dtype, down = {"e4m3": (ml_dtypes.float8_e4m3fn, 7), "e5m2": (ml_dtypes.float8_e5m2, 14)}[fmt]
    v = np.moveaxis(np.asarray(x, np.float32).astype(ml_dtypes.bfloat16).astype(np.float64), axis, -1)
    blocks = v.reshape(v.shape[:-1] + (-1, 32))
    amax = np.abs(blocks).max(-1, keepdims=True)
    byte = np.maximum(np.where(amax > 0, np.frexp(amax)[1] - 1 + 127, 0) - down, 1)
    scale = np.exp2(byte - 127.0)
    codes = (blocks / scale).astype(np.float32).astype(dtype).astype(np.float64)
    return np.moveaxis((codes * scale).reshape(v.shape), -1, axis)


WIDE = False


def mx_kscale(k):
    if not WIDE:
        return np.ones(k)
    levels = np.array([10, -10, 5, -5, 0])
    a = np.random.permutation(np.resize(levels, k // 512 * 4)).reshape(k // 512, 4)
    idx = np.arange(k)
    return np.exp2(a[idx // 512, idx % 128 // 32])


BF16 = ml_dtypes.bfloat16


def bf(x):
    return np.asarray(x, np.float32).astype(BF16)


def f64(x):
    return np.asarray(x).astype(np.float64)


B, L, H, G, DEPTH = 64, 64, 512, 256, 3
EPS = 1e-5


def layernorm(v, g, b):
    mu = v.mean(-1, keepdims=True)
    var = np.square(v - mu).mean(-1, keepdims=True)
    return (v - mu) / np.sqrt(var + EPS) * g + b


def setup_inputs():
    s, t = mx_kscale(H), mx_kscale(H)
    return {"x_nodes": bf(np.random.standard_normal((B, L, H)) * s),
            "w1": bf(np.random.standard_normal((H, H)) / np.sqrt(H) / s[:, None]),
            "b1": bf(np.random.standard_normal(H) * 0.3),
            "gamma": bf((1.0 + 0.1 * np.random.standard_normal(H)) * t),
            "beta": bf(0.2 * np.random.standard_normal(H) * t),
            "w2": bf(np.random.standard_normal((H, G)) / np.sqrt(H) / t[:, None]),
            "b2": bf(np.random.standard_normal(G) * 0.3)}


def reference(x_nodes, w1, b1, gamma, beta, w2, b2):
    h = (mxq(f64(x_nodes), 2, "e4m3") @ mxq(f64(w1), 0, "e4m3")) + f64(b1)
    r = np.maximum(layernorm(h, f64(gamma), f64(beta)), 0.0)
    x1 = (mxq(r, 2, "e4m3") @ mxq(f64(w2), 0, "e4m3")) + f64(b2)
    x2 = np.broadcast_to(x1.max(axis=1, keepdims=True), x1.shape)
    x = np.concatenate([x1, x2], axis=2)
    return x.max(axis=1)

@@ -1,0 +1,299 @@
+from contextlib import ExitStack
+
+import concourse.masks as masks
+import concourse.mybir as mybir
+
+F32 = mybir.dt.float32
+BF16 = mybir.dt.bfloat16
+U32 = mybir.dt.uint32
+U8 = mybir.dt.uint8
+FP8X4 = mybir.dt.float8_e4m3fn_x4
+ALU = mybir.AluOpType
+ACT = mybir.ActivationFunctionType
+AXIS = mybir.AxisListType
+
+P = 128
+PACK = 4
+POLYLINES = 64
+NODES = 64
+H = 512
+G = 256
+EPS = 1e-5
+TOKENS = POLYLINES * NODES
+TILES = 2
+UNIT = TILES * P
+UNITS = TOKENS // UNIT
+H_CHUNKS = H // P
+G_CHUNKS = G // P
+LINES_PER_UNIT = UNIT // NODES
+WORDS = H // 2
+LAST_LAG = 6
+W2_ROUND = 1
+
+FLOPS = 2 * TOKENS * H * H + 2 * TOKENS * H * G
+
+
+def quantise_weight(nc, pool, raw, width, label):
+    grouped = pool.tile([P, width, PACK], BF16, name=label + "_grouped", align_bytes=64)
+    codes = pool.tile([P, width], U32, name=label + "_codes", align_bytes=64)
+    scales = pool.tile([P, width], U8, name=label + "_scales", align_bytes=64)
+    nc.vector.tensor_copy(out=grouped[:], in_=raw[:].rearrange("p t c -> p c t"))
+    nc.vector.quantize_mx(
+        out=codes[:].bitcast(FP8X4),
+        scales=scales[:],
+        in_=grouped[:].rearrange("p c t -> p (c t)"),
+    )
+    return codes, scales
+
+
+def tile_sub_graph_pb_kernel(tc, x_nodes, w1, b1, gamma, beta, w2, b2, out):
+    nc = tc.nc
+    x_flat = x_nodes.rearrange("b l k -> (b l) k")
+
+    with ExitStack() as ctx:
+        ctx.enter_context(tc.manual_schedule())
+        const = ctx.enter_context(tc.tile_pool(name="const", bufs=1))
+        x_pool = ctx.enter_context(tc.tile_pool(name="x", bufs=UNITS))
+        two = ctx.enter_context(tc.tile_pool(name="two", bufs=2))
+        three = ctx.enter_context(tc.tile_pool(name="three", bufs=3))
+        psum_x = ctx.enter_context(tc.psum_pool(name="psum_x", bufs=1))
+        psum_h = ctx.enter_context(tc.psum_pool(name="psum_h", bufs=TILES))
+        psum_z = ctx.enter_context(tc.psum_pool(name="psum_z", bufs=4))
+        psum_x1 = ctx.enter_context(tc.psum_pool(name="psum_x1", bufs=1))
+
+        b1_row = const.tile([P, H], BF16)
+        nc.vector.memset(b1_row[:], 0.0)
+        nc.scalar.dma_start(out=b1_row[0:1, :], in_=b1.rearrange("(o c) -> o c", o=1))
+        rows_bf = const.tile([P, P], BF16)
+        nc.vector.memset(rows_bf[:], 0.0)
+        nc.scalar.dma_start(out=rows_bf[0:4, :], in_=gamma.rearrange("(t p) -> t p", p=P))
+        nc.scalar.dma_start(out=rows_bf[4:8, :], in_=beta.rearrange("(t p) -> t p", p=P))
+        nc.scalar.dma_start(out=rows_bf[8:10, :], in_=b2.rearrange("(t p) -> t p", p=P))
+        w1_raw = const.tile([P, PACK, H], BF16)
+        for u in range(2):
+            nc.scalar.dma_start(
+                out=w1_raw[:, 2 * u : 2 * u + 2, :],
+                in_=w1[256 * u : 256 * u + 256, :].rearrange("(q e) c -> q e c", e=2),
+            )
+        w2_raw = const.tile([P, PACK, G], BF16)
+        nc.scalar.dma_start(out=w2_raw[:], in_=w2.rearrange("(t p) c -> p t c", p=P))
+        x_sb = {}
+        for unit in range(UNITS):
+            x_sb[unit] = x_pool.tile([P, TILES * H], BF16, name="x_sb")
+            nc.sync.dma_start(
+                out=x_sb[unit][:].rearrange("p (i k) -> p i k", i=TILES),
+                in_=x_flat[unit * UNIT : (unit + 1) * UNIT, :].rearrange("(i p) k -> p i k", p=P),
+            )
+
+        eps_col = const.tile([P, 1], F32)
+        nc.vector.memset(eps_col[:], EPS)
+        warm = const.tile([P, 1], F32)
+        nc.scalar.activation(out=warm[:], in_=eps_col[:], func=ACT.Sqrt)
+        ident = const.tile([P, P], F32)
+        masks.make_identity(nc, ident[:])
+        ones = const.tile([P, P], BF16)
+        nc.vector.memset(ones[:], 1.0)
+        best = const.tile([P, G_CHUNKS, P], F32)
+        nc.vector.memset(best[:], 0.0)
+
+        b1_ps = psum_h.tile([P, H], F32, tag="h_ps")
+        nc.tensor.matmul(out=b1_ps[:], lhsT=ones[:], rhs=b1_row[:], start=True, stop=True)
+        b1_all = const.tile([P, H], F32)
+        nc.scalar.copy(out=b1_all[:], in_=b1_ps[:])
+        rows_f32 = const.tile([P, P], F32)
+        nc.vector.tensor_copy(out=rows_f32[:], in_=rows_bf[:])
+        cols_ps = psum_h.tile([P, P], F32, tag="h_ps")
+        nc.tensor.transpose(out=cols_ps[:], in_=rows_f32[:], identity=ident[:])
+        cols = const.tile([P, 16], F32)
+        nc.vector.tensor_copy(out=cols[:], in_=cols_ps[:, 0:16])
+
+        kept = {}
+
+        def transpose_x(unit):
+            x_words = x_sb[unit][:].bitcast(F32)
+            xT = psum_x.tile([P, 2, UNIT], F32, tag="xT")
+            for i in range(TILES):
+                for u in range(2):
+                    nc.tensor.transpose(
+                        out=xT[:, u, i * P : (i + 1) * P],
+                        in_=x_words[:, WORDS * i + P * u : WORDS * i + P * (u + 1)],
+                        identity=ident[:],
+                    )
+            kept["xT", unit] = xT
+
+        def group_x(unit):
+            x_grouped = two.tile([P, UNIT * PACK], BF16, align_bytes=64)
+            nc.scalar.copy(
+                out=x_grouped[:].bitcast(F32).rearrange("p (c u) -> p c u", u=2),
+                in_=kept["xT", unit][:].rearrange("p u c -> p c u"),
+            )
+            kept["x_grouped", unit] = x_grouped
+
+        def quantise_x(unit):
+            x_codes = two.tile([P, UNIT], U32, align_bytes=64)
+            x_scales = two.tile([P, UNIT], U8, align_bytes=64)
+            nc.vector.quantize_mx(
+                out=x_codes[:].bitcast(FP8X4), scales=x_scales[:], in_=kept["x_grouped", unit][:]
+            )
+            kept["x_codes", unit] = x_codes
+            kept["x_scales", unit] = x_scales
+
+        def multiply_w1(unit):
+            for i in range(TILES):
+                h_ps = psum_h.tile([P, H], F32, tag="h_ps")
+                nc.tensor.matmul_mx(
+                    out=h_ps[:],
+                    lhsT=kept["x_codes", unit][:, i * P : (i + 1) * P].bitcast(FP8X4),
+                    lhsT_scale=kept["x_scales", unit][:, i * P : (i + 1) * P],
+                    rhs=w1_codes[:].bitcast(FP8X4),
+                    rhs_scale=w1_scales[:],
+                    start=True,
+                    stop=True,
+                )
+                kept["h_ps", unit, i] = h_ps
+
+        def add_b1(unit):
+            h = three.tile([P, TILES, H], F32)
+            h_sum = two.tile([P, TILES], F32)
+            for i in range(TILES):
+                nc.vector.scalar_tensor_tensor(
+                    out=h[:, i, :],
+                    in0=kept["h_ps", unit, i][:],
+                    scalar=1.0,
+                    in1=b1_all[:],
+                    op0=ALU.mult,
+                    op1=ALU.add,
+                    accum_out=h_sum[:, i : i + 1],
+                )
+            neg_mean = three.tile([P, TILES], F32)
+            nc.vector.tensor_scalar_mul(out=neg_mean[:], in0=h_sum[:], scalar1=-1.0 / H)
+            kept["h", unit] = h
+            kept["neg_mean", unit] = neg_mean
+
+        def deviation(unit):
+            sq_sum = two.tile([P, TILES], F32)
+            for i in range(TILES):
+                squares = two.tile([P, H], BF16)
+                nc.scalar.activation(
+                    out=squares[:],
+                    in_=kept["h", unit][:, i, :],
+                    func=ACT.Square,
+                    bias=kept["neg_mean", unit][:, i : i + 1],
+                    accum_out=sq_sum[:, i : i + 1],
+                )
+            std = two.tile([P, TILES], F32)
+            nc.scalar.activation(out=std[:], in_=sq_sum[:], func=ACT.Sqrt, bias=eps_col[:], scale=1.0 / H)
+            kept["std", unit] = std
+
+        def normalise(unit):
+            inv_std = two.tile([P, TILES], F32)
+            nc.vector.reciprocal(out=inv_std[:], in_=kept["std", unit][:])
+            z = two.tile([P, TILES, H], F32)
+            for i in range(TILES):
+                nc.vector.tensor_scalar(
+                    out=z[:, i, :],
+                    in0=kept["h", unit][:, i, :],
+                    scalar1=kept["neg_mean", unit][:, i : i + 1],
+                    scalar2=inv_std[:, i : i + 1],
+                    op0=ALU.add,
+                    op1=ALU.mult,
+                )
+            kept["z", unit] = z
+
+        def transpose_z(unit):
+            for bank in range(2):
+                zT = psum_z.tile([P, 2, UNIT], F32, tag="zT")
+                for s in range(2):
+                    t = 2 * bank + s
+                    for i in range(TILES):
+                        nc.tensor.transpose(
+                            out=zT[:, s, i * P : (i + 1) * P],
+                            in_=kept["z", unit][:, i, t * P : (t + 1) * P],
+                            identity=ident[:],
+                        )
+                kept["zT", unit, bank] = zT
+
+        def scale_relu(unit):
+            r_planes = two.tile([P, H_CHUNKS, UNIT], BF16)
+            for t in range(H_CHUNKS):
+                nc.scalar.activation(
+                    out=r_planes[:, t, :],
+                    in_=kept["zT", unit, t // 2][:, t % 2, :],
+                    func=ACT.Relu,
+                    bias=cols[:, 4 + t : 5 + t],
+                    scale=cols[:, t : t + 1],
+                )
+            kept["r_planes", unit] = r_planes
+
+        def group_r(unit):
+            r_grouped = two.tile([P, UNIT, PACK], BF16, align_bytes=64)
+            nc.vector.tensor_copy(out=r_grouped[:], in_=kept["r_planes", unit][:].rearrange("p t c -> p c t"))
+            kept["r_grouped", unit] = r_grouped
+
+        def quantise_r(unit):
+            r_codes = two.tile([P, UNIT], U32, align_bytes=64)
+            r_scales = two.tile([P, UNIT], U8, align_bytes=64)
+            nc.vector.quantize_mx(
+                out=r_codes[:].bitcast(FP8X4),
+                scales=r_scales[:],
+                in_=kept["r_grouped", unit][:].rearrange("p c t -> p (c t)"),
+            )
+            kept["r_codes", unit] = r_codes
+            kept["r_scales", unit] = r_scales
+
+        def multiply_w2(unit):
+            x1_ps = psum_x1.tile([P, G_CHUNKS, UNIT], F32, tag="x1_ps")
+            for c in range(G_CHUNKS):
+                nc.tensor.matmul_mx(
+                    out=x1_ps[:, c, :],
+                    lhsT=w2_codes[:, c * P : (c + 1) * P].bitcast(FP8X4),
+                    lhsT_scale=w2_scales[:, c * P : (c + 1) * P],
+                    rhs=kept["r_codes", unit][:].bitcast(FP8X4),
+                    rhs_scale=kept["r_scales", unit][:],
+                    start=True,
+                    stop=True,
+                )
+            kept["x1_ps", unit] = x1_ps
+
+        def take_max(unit):
+            nc.vector.tensor_reduce(
+                out=best[:, :, unit * LINES_PER_UNIT : (unit + 1) * LINES_PER_UNIT],
+                in_=kept["x1_ps", unit][:].rearrange("m c (b l) -> m c b l", l=NODES),
+                axis=AXIS.X,
+                op=ALU.max,
+            )
+
+        def at(step, unit):
+            if 0 <= unit < UNITS:
+                step(unit)
+
+        transpose_x(0)
+        w1_codes, w1_scales = quantise_weight(nc, const, w1_raw, H, "w1")
+        w2_codes, w2_scales = None, None
+        for now in range(UNITS + LAST_LAG):
+            at(quantise_x, now - 1)
+            if now == W2_ROUND:
+                w2_codes, w2_scales = quantise_weight(nc, const, w2_raw, G, "w2")
+            at(quantise_r, now - 6)
+            at(multiply_w2, now - 6)
+            at(normalise, now - 4)
+            at(group_x, now)
+            at(add_b1, now - 2)
+            at(transpose_z, now - 4)
+            at(transpose_x, now + 1)
+            at(multiply_w1, now - 1)
+            at(scale_relu, now - 5)
+            at(take_max, now - 6)
+            at(deviation, now - 3)
+            at(group_r, now - 5)
+
+        outT = psum_x.tile([P, G_CHUNKS, P], F32, tag="xT")
+        for c in range(G_CHUNKS):
+            nc.vector.tensor_scalar_add(
+                out=best[:, c, 0:POLYLINES], in0=best[:, c, 0:POLYLINES], scalar1=cols[:, 8 + c : 9 + c]
+            )
+            nc.tensor.transpose(out=outT[:, c, :], in_=best[:, c, :], identity=ident[:])
+        out_sb = const.tile([P, G], F32)
+        nc.vector.tensor_copy(out=out_sb[:], in_=outT[:].rearrange("b c m -> b (c m)"))
+        nc.sync.dma_start(out=out[:, 0:G], in_=out_sb[0:POLYLINES, :])
+        nc.sync.dma_start(out=out[:, G : 2 * G], in_=out_sb[0:POLYLINES, :])

@@ -27,7 +27,7 @@ H_CHUNKS = H // P
 G_CHUNKS = G // P
 LINES_PER_UNIT = UNIT // NODES
 WORDS = H // 2
-LAST_LAG = 6
+LAST_LAG = 7
 W2_ROUND = 1
 
 FLOPS = 2 * TOKENS * H * H + 2 * TOKENS * H * G
@@ -185,16 +185,19 @@ def tile_sub_graph_pb_kernel(tc, x_nodes, w1, b1, gamma, beta, w2, b2, out):
             nc.scalar.activation(out=std[:], in_=sq_sum[:], func=ACT.Sqrt, bias=eps_col[:], scale=1.0 / H)
             kept["std", unit] = std
 
-        def normalise(unit):
+        def invert_std(unit):
             inv_std = two.tile([P, TILES], F32)
             nc.vector.reciprocal(out=inv_std[:], in_=kept["std", unit][:])
+            kept["inv_std", unit] = inv_std
+
+        def normalise(unit):
             z = two.tile([P, TILES, H], F32)
             for i in range(TILES):
-                nc.vector.tensor_scalar(
+                nc.gpsimd.tensor_scalar(
                     out=z[:, i, :],
                     in0=kept["h", unit][:, i, :],
                     scalar1=kept["neg_mean", unit][:, i : i + 1],
-                    scalar2=inv_std[:, i : i + 1],
+                    scalar2=kept["inv_std", unit][:, i : i + 1],
                     op0=ALU.add,
                     op1=ALU.mult,
                 )
@@ -274,18 +277,19 @@ def tile_sub_graph_pb_kernel(tc, x_nodes, w1, b1, gamma, beta, w2, b2, out):
             at(quantise_x, now - 1)
             if now == W2_ROUND:
                 w2_codes, w2_scales = quantise_weight(nc, const, w2_raw, G, "w2")
+            at(invert_std, now - 4)
+            at(normalise, now - 4)
+            at(add_b1, now - 2)
+            at(multiply_w1, now - 1)
+            at(group_x, now)
+            at(transpose_x, now + 1)
+            at(transpose_z, now - 4)
+            at(take_max, now - 7)
             at(quantise_r, now - 6)
             at(multiply_w2, now - 6)
-            at(normalise, now - 4)
-            at(group_x, now)
-            at(add_b1, now - 2)
-            at(transpose_z, now - 4)
-            at(transpose_x, now + 1)
-            at(multiply_w1, now - 1)
             at(scale_relu, now - 5)
-            at(take_max, now - 6)
-            at(deviation, now - 3)
             at(group_r, now - 5)
+            at(deviation, now - 3)
 
         outT = psum_x.tile([P, G_CHUNKS, P], F32, tag="xT")
         for c in range(G_CHUNKS):

@@ -27,8 +27,9 @@ H_CHUNKS = H // P
 G_CHUNKS = G // P
 LINES_PER_UNIT = UNIT // NODES
 WORDS = H // 2
-LAST_LAG = 7
-W2_ROUND = 1
+LAST_LAG = 8
+FIRST_PRODUCT = 1
+RUN = 4
 
 FLOPS = 2 * TOKENS * H * H + 2 * TOKENS * H * G
 
@@ -37,7 +38,10 @@ def quantise_weight(nc, pool, raw, width, label):
     grouped = pool.tile([P, width, PACK], BF16, name=label + "_grouped", align_bytes=64)
     codes = pool.tile([P, width], U32, name=label + "_codes", align_bytes=64)
     scales = pool.tile([P, width], U8, name=label + "_scales", align_bytes=64)
-    nc.vector.tensor_copy(out=grouped[:], in_=raw[:].rearrange("p t c -> p c t"))
+    nc.vector.tensor_copy(
+        out=grouped[:].rearrange("p (c i) t -> p c t i", i=RUN),
+        in_=raw[:].rearrange("p t (c i) -> p c t i", i=RUN),
+    )
     nc.vector.quantize_mx(
         out=codes[:].bitcast(FP8X4),
         scales=scales[:],
@@ -57,10 +61,31 @@ def tile_sub_graph_pb_kernel(tc, x_nodes, w1, b1, gamma, beta, w2, b2, out):
         two = ctx.enter_context(tc.tile_pool(name="two", bufs=2))
         three = ctx.enter_context(tc.tile_pool(name="three", bufs=3))
         psum_x = ctx.enter_context(tc.psum_pool(name="psum_x", bufs=1))
-        psum_h = ctx.enter_context(tc.psum_pool(name="psum_h", bufs=TILES))
-        psum_z = ctx.enter_context(tc.psum_pool(name="psum_z", bufs=4))
+        psum_h = ctx.enter_context(tc.psum_pool(name="psum_h", bufs=2 * TILES))
+        psum_z = ctx.enter_context(tc.psum_pool(name="psum_z", bufs=2))
         psum_x1 = ctx.enter_context(tc.psum_pool(name="psum_x1", bufs=1))
 
+        x_sb = {}
+
+        def load_x(unit):
+            x_sb[unit] = x_pool.tile([P, TILES * H], BF16, name="x_sb")
+            nc.sync.dma_start(
+                out=x_sb[unit][:].rearrange("p (i k) -> p i k", i=TILES),
+                in_=x_flat[unit * UNIT : (unit + 1) * UNIT, :].rearrange("(i p) k -> p i k", p=P),
+            )
+
+        load_x(0)
+        w1_raw = const.tile([P, PACK, H], BF16)
+        for u in range(2):
+            nc.scalar.dma_start(
+                out=w1_raw[:, 2 * u : 2 * u + 2, :],
+                in_=w1[256 * u : 256 * u + 256, :].rearrange("(q e) c -> q e c", e=2),
+            )
+        load_x(1)
+        eps_col = const.tile([P, 1], F32)
+        nc.vector.memset(eps_col[:], EPS)
+        warm = const.tile([P, 1], F32)
+        nc.scalar.activation(out=warm[:], in_=eps_col[:], func=ACT.Sqrt)
         b1_row = const.tile([P, H], BF16)
         nc.vector.memset(b1_row[:], 0.0)
         nc.scalar.dma_start(out=b1_row[0:1, :], in_=b1.rearrange("(o c) -> o c", o=1))
@@ -69,43 +94,29 @@ def tile_sub_graph_pb_kernel(tc, x_nodes, w1, b1, gamma, beta, w2, b2, out):
         nc.scalar.dma_start(out=rows_bf[0:4, :], in_=gamma.rearrange("(t p) -> t p", p=P))
         nc.scalar.dma_start(out=rows_bf[4:8, :], in_=beta.rearrange("(t p) -> t p", p=P))
         nc.scalar.dma_start(out=rows_bf[8:10, :], in_=b2.rearrange("(t p) -> t p", p=P))
-        w1_raw = const.tile([P, PACK, H], BF16)
-        for u in range(2):
-            nc.scalar.dma_start(
-                out=w1_raw[:, 2 * u : 2 * u + 2, :],
-                in_=w1[256 * u : 256 * u + 256, :].rearrange("(q e) c -> q e c", e=2),
-            )
         w2_raw = const.tile([P, PACK, G], BF16)
         nc.scalar.dma_start(out=w2_raw[:], in_=w2.rearrange("(t p) c -> p t c", p=P))
-        x_sb = {}
-        for unit in range(UNITS):
-            x_sb[unit] = x_pool.tile([P, TILES * H], BF16, name="x_sb")
-            nc.sync.dma_start(
-                out=x_sb[unit][:].rearrange("p (i k) -> p i k", i=TILES),
-                in_=x_flat[unit * UNIT : (unit + 1) * UNIT, :].rearrange("(i p) k -> p i k", p=P),
-            )
+        for unit in range(2, UNITS):
+            load_x(unit)
 
-        eps_col = const.tile([P, 1], F32)
-        nc.vector.memset(eps_col[:], EPS)
-        warm = const.tile([P, 1], F32)
-        nc.scalar.activation(out=warm[:], in_=eps_col[:], func=ACT.Sqrt)
         ident = const.tile([P, P], F32)
         masks.make_identity(nc, ident[:])
         ones = const.tile([P, P], BF16)
         nc.vector.memset(ones[:], 1.0)
         best = const.tile([P, G_CHUNKS, P], F32)
         nc.vector.memset(best[:], 0.0)
-
-        b1_ps = psum_h.tile([P, H], F32, tag="h_ps")
-        nc.tensor.matmul(out=b1_ps[:], lhsT=ones[:], rhs=b1_row[:], start=True, stop=True)
         b1_all = const.tile([P, H], F32)
-        nc.scalar.copy(out=b1_all[:], in_=b1_ps[:])
-        rows_f32 = const.tile([P, P], F32)
-        nc.vector.tensor_copy(out=rows_f32[:], in_=rows_bf[:])
-        cols_ps = psum_h.tile([P, P], F32, tag="h_ps")
-        nc.tensor.transpose(out=cols_ps[:], in_=rows_f32[:], identity=ident[:])
         cols = const.tile([P, 16], F32)
-        nc.vector.tensor_copy(out=cols[:], in_=cols_ps[:, 0:16])
+
+        def spread_vectors():
+            b1_ps = psum_z.tile([P, H], F32, tag="zT")
+            nc.tensor.matmul(out=b1_ps[:], lhsT=ones[:], rhs=b1_row[:], start=True, stop=True)
+            nc.scalar.copy(out=b1_all[:], in_=b1_ps[:])
+            rows_f32 = const.tile([P, P], F32)
+            nc.vector.tensor_copy(out=rows_f32[:], in_=rows_bf[:])
+            cols_ps = psum_z.tile([P, P], F32, tag="zT")
+            nc.tensor.transpose(out=cols_ps[:], in_=rows_f32[:], identity=ident[:])
+            nc.vector.tensor_copy(out=cols[:], in_=cols_ps[:, 0:16])
 
         kept = {}
 
@@ -230,7 +241,10 @@ def tile_sub_graph_pb_kernel(tc, x_nodes, w1, b1, gamma, beta, w2, b2, out):
 
         def group_r(unit):
             r_grouped = two.tile([P, UNIT, PACK], BF16, align_bytes=64)
-            nc.vector.tensor_copy(out=r_grouped[:], in_=kept["r_planes", unit][:].rearrange("p t c -> p c t"))
+            nc.vector.tensor_copy(
+                out=r_grouped[:].rearrange("p (c i) t -> p c t i", i=RUN),
+                in_=kept["r_planes", unit][:].rearrange("p t (c i) -> p c t i", i=RUN),
+            )
             kept["r_grouped", unit] = r_grouped
 
         def quantise_r(unit):
@@ -271,25 +285,27 @@ def tile_sub_graph_pb_kernel(tc, x_nodes, w1, b1, gamma, beta, w2, b2, out):
                 step(unit)
 
         transpose_x(0)
-        w1_codes, w1_scales = quantise_weight(nc, const, w1_raw, H, "w1")
-        w2_codes, w2_scales = None, None
+        w1_codes, w1_scales, w2_codes, w2_scales = None, None, None, None
         for now in range(UNITS + LAST_LAG):
             at(quantise_x, now - 1)
-            if now == W2_ROUND:
-                w2_codes, w2_scales = quantise_weight(nc, const, w2_raw, G, "w2")
+            at(quantise_r, now - 7)
+            if now == FIRST_PRODUCT:
+                w1_codes, w1_scales = quantise_weight(nc, const, w1_raw, H, "w1")
             at(invert_std, now - 4)
             at(normalise, now - 4)
-            at(add_b1, now - 2)
-            at(multiply_w1, now - 1)
+            at(transpose_z, now - 5)
             at(group_x, now)
             at(transpose_x, now + 1)
-            at(transpose_z, now - 4)
-            at(take_max, now - 7)
-            at(quantise_r, now - 6)
-            at(multiply_w2, now - 6)
-            at(scale_relu, now - 5)
-            at(group_r, now - 5)
+            at(multiply_w1, now - 1)
+            at(take_max, now - 8)
+            at(multiply_w2, now - 7)
+            at(add_b1, now - 2)
             at(deviation, now - 3)
+            at(scale_relu, now - 5)
+            at(group_r, now - 6)
+            if now == FIRST_PRODUCT:
+                spread_vectors()
+                w2_codes, w2_scales = quantise_weight(nc, const, w2_raw, G, "w2")
 
         outT = psum_x.tile([P, G_CHUNKS, P], F32, tag="xT")
         for c in range(G_CHUNKS):

@@ -28,26 +28,24 @@ G_CHUNKS = G // P
 LINES_PER_UNIT = UNIT // NODES
 WORDS = H // 2
 LAST_LAG = 8
-FIRST_PRODUCT = 1
 RUN = 4
 
 FLOPS = 2 * TOKENS * H * H + 2 * TOKENS * H * G
 
 
-def quantise_weight(nc, pool, raw, width, label):
-    grouped = pool.tile([P, width, PACK], BF16, name=label + "_grouped", align_bytes=64)
-    codes = pool.tile([P, width], U32, name=label + "_codes", align_bytes=64)
-    scales = pool.tile([P, width], U8, name=label + "_scales", align_bytes=64)
-    nc.vector.tensor_copy(
+def group_words(copy, grouped, planes):
+    copy(
         out=grouped[:].rearrange("p (c i) t -> p c t i", i=RUN),
-        in_=raw[:].rearrange("p t (c i) -> p c t i", i=RUN),
+        in_=planes[:].rearrange("p t (c i) -> p c t i", i=RUN),
     )
+
+
+def quantise(nc, codes, scales, grouped):
     nc.vector.quantize_mx(
         out=codes[:].bitcast(FP8X4),
         scales=scales[:],
         in_=grouped[:].rearrange("p c t -> p (c t)"),
     )
-    return codes, scales
 
 
 def tile_sub_graph_pb_kernel(tc, x_nodes, w1, b1, gamma, beta, w2, b2, out):
@@ -82,10 +80,6 @@ def tile_sub_graph_pb_kernel(tc, x_nodes, w1, b1, gamma, beta, w2, b2, out):
                 in_=w1[256 * u : 256 * u + 256, :].rearrange("(q e) c -> q e c", e=2),
             )
         load_x(1)
-        eps_col = const.tile([P, 1], F32)
-        nc.vector.memset(eps_col[:], EPS)
-        warm = const.tile([P, 1], F32)
-        nc.scalar.activation(out=warm[:], in_=eps_col[:], func=ACT.Sqrt)
         b1_row = const.tile([P, H], BF16)
         nc.vector.memset(b1_row[:], 0.0)
         nc.scalar.dma_start(out=b1_row[0:1, :], in_=b1.rearrange("(o c) -> o c", o=1))
@@ -94,6 +88,10 @@ def tile_sub_graph_pb_kernel(tc, x_nodes, w1, b1, gamma, beta, w2, b2, out):
         nc.scalar.dma_start(out=rows_bf[0:4, :], in_=gamma.rearrange("(t p) -> t p", p=P))
         nc.scalar.dma_start(out=rows_bf[4:8, :], in_=beta.rearrange("(t p) -> t p", p=P))
         nc.scalar.dma_start(out=rows_bf[8:10, :], in_=b2.rearrange("(t p) -> t p", p=P))
+        eps_col = const.tile([P, 1], F32)
+        nc.vector.memset(eps_col[:], EPS)
+        warm = const.tile([P, 1], F32)
+        nc.scalar.activation(out=warm[:], in_=eps_col[:], func=ACT.Sqrt)
         w2_raw = const.tile([P, PACK, G], BF16)
         nc.scalar.dma_start(out=w2_raw[:], in_=w2.rearrange("(t p) c -> p t c", p=P))
         for unit in range(2, UNITS):
@@ -108,15 +106,24 @@ def tile_sub_graph_pb_kernel(tc, x_nodes, w1, b1, gamma, beta, w2, b2, out):
         b1_all = const.tile([P, H], F32)
         cols = const.tile([P, 16], F32)
 
-        def spread_vectors():
+        w1_grouped = const.tile([P, H, PACK], BF16, align_bytes=64)
+        w1_codes = const.tile([P, H], U32, align_bytes=64)
+        w1_scales = const.tile([P, H], U8, align_bytes=64)
+        w2_grouped = const.tile([P, G, PACK], BF16, align_bytes=64)
+        w2_codes = const.tile([P, G], U32, align_bytes=64)
+        w2_scales = const.tile([P, G], U8, align_bytes=64)
+
+        def spread_b1():
             b1_ps = psum_z.tile([P, H], F32, tag="zT")
             nc.tensor.matmul(out=b1_ps[:], lhsT=ones[:], rhs=b1_row[:], start=True, stop=True)
             nc.scalar.copy(out=b1_all[:], in_=b1_ps[:])
+
+        def turn_vectors():
             rows_f32 = const.tile([P, P], F32)
-            nc.vector.tensor_copy(out=rows_f32[:], in_=rows_bf[:])
+            nc.scalar.copy(out=rows_f32[:], in_=rows_bf[:])
             cols_ps = psum_z.tile([P, P], F32, tag="zT")
             nc.tensor.transpose(out=cols_ps[:], in_=rows_f32[:], identity=ident[:])
-            nc.vector.tensor_copy(out=cols[:], in_=cols_ps[:, 0:16])
+            nc.scalar.copy(out=cols[:], in_=cols_ps[:, 0:16])
 
         kept = {}
 
@@ -133,9 +140,9 @@ def tile_sub_graph_pb_kernel(tc, x_nodes, w1, b1, gamma, beta, w2, b2, out):
             kept["xT", unit] = xT
 
         def group_x(unit):
-            x_grouped = two.tile([P, UNIT * PACK], BF16, align_bytes=64)
+            x_grouped = two.tile([P, UNIT, PACK], BF16, align_bytes=64)
             nc.scalar.copy(
-                out=x_grouped[:].bitcast(F32).rearrange("p (c u) -> p c u", u=2),
+                out=x_grouped[:].rearrange("p c t -> p (c t)").bitcast(F32).rearrange("p (c u) -> p c u", u=2),
                 in_=kept["xT", unit][:].rearrange("p u c -> p c u"),
             )
             kept["x_grouped", unit] = x_grouped
@@ -143,9 +150,7 @@ def tile_sub_graph_pb_kernel(tc, x_nodes, w1, b1, gamma, beta, w2, b2, out):
         def quantise_x(unit):
             x_codes = two.tile([P, UNIT], U32, align_bytes=64)
             x_scales = two.tile([P, UNIT], U8, align_bytes=64)
-            nc.vector.quantize_mx(
-                out=x_codes[:].bitcast(FP8X4), scales=x_scales[:], in_=kept["x_grouped", unit][:]
-            )
+            quantise(nc, x_codes, x_scales, kept["x_grouped", unit])
             kept["x_codes", unit] = x_codes
             kept["x_scales", unit] = x_scales
 
@@ -176,12 +181,15 @@ def tile_sub_graph_pb_kernel(tc, x_nodes, w1, b1, gamma, beta, w2, b2, out):
                     op1=ALU.add,
                     accum_out=h_sum[:, i : i + 1],
                 )
-            neg_mean = three.tile([P, TILES], F32)
-            nc.vector.tensor_scalar_mul(out=neg_mean[:], in0=h_sum[:], scalar1=-1.0 / H)
             kept["h", unit] = h
+            kept["h_sum", unit] = h_sum
+
+        def negate_mean(unit):
+            neg_mean = three.tile([P, TILES], F32)
+            nc.vector.tensor_scalar_mul(out=neg_mean[:], in0=kept["h_sum", unit][:], scalar1=-1.0 / H)
             kept["neg_mean", unit] = neg_mean
 
-        def deviation(unit):
+        def sum_squares(unit):
             sq_sum = two.tile([P, TILES], F32)
             for i in range(TILES):
                 squares = two.tile([P, H], BF16)
@@ -192,8 +200,13 @@ def tile_sub_graph_pb_kernel(tc, x_nodes, w1, b1, gamma, beta, w2, b2, out):
                     bias=kept["neg_mean", unit][:, i : i + 1],
                     accum_out=sq_sum[:, i : i + 1],
                 )
+            kept["sq_sum", unit] = sq_sum
+
+        def take_root(unit):
             std = two.tile([P, TILES], F32)
-            nc.scalar.activation(out=std[:], in_=sq_sum[:], func=ACT.Sqrt, bias=eps_col[:], scale=1.0 / H)
+            nc.scalar.activation(
+                out=std[:], in_=kept["sq_sum", unit][:], func=ACT.Sqrt, bias=eps_col[:], scale=1.0 / H
+            )
             kept["std", unit] = std
 
         def invert_std(unit):
@@ -241,20 +254,13 @@ def tile_sub_graph_pb_kernel(tc, x_nodes, w1, b1, gamma, beta, w2, b2, out):
 
         def group_r(unit):
             r_grouped = two.tile([P, UNIT, PACK], BF16, align_bytes=64)
-            nc.vector.tensor_copy(
-                out=r_grouped[:].rearrange("p (c i) t -> p c t i", i=RUN),
-                in_=kept["r_planes", unit][:].rearrange("p t (c i) -> p c t i", i=RUN),
-            )
+            group_words(nc.vector.tensor_copy, r_grouped, kept["r_planes", unit])
             kept["r_grouped", unit] = r_grouped
 
         def quantise_r(unit):
             r_codes = two.tile([P, UNIT], U32, align_bytes=64)
             r_scales = two.tile([P, UNIT], U8, align_bytes=64)
-            nc.vector.quantize_mx(
-                out=r_codes[:].bitcast(FP8X4),
-                scales=r_scales[:],
-                in_=kept["r_grouped", unit][:].rearrange("p c t -> p (c t)"),
-            )
+            quantise(nc, r_codes, r_scales, kept["r_grouped", unit])
             kept["r_codes", unit] = r_codes
             kept["r_scales", unit] = r_scales
 
@@ -285,27 +291,33 @@ def tile_sub_graph_pb_kernel(tc, x_nodes, w1, b1, gamma, beta, w2, b2, out):
                 step(unit)
 
         transpose_x(0)
-        w1_codes, w1_scales, w2_codes, w2_scales = None, None, None, None
         for now in range(UNITS + LAST_LAG):
-            at(quantise_x, now - 1)
-            at(quantise_r, now - 7)
-            if now == FIRST_PRODUCT:
-                w1_codes, w1_scales = quantise_weight(nc, const, w1_raw, H, "w1")
+            at(multiply_w1, now - 1)
             at(invert_std, now - 4)
             at(normalise, now - 4)
-            at(transpose_z, now - 5)
+            at(sum_squares, now - 3)
             at(group_x, now)
-            at(transpose_x, now + 1)
-            at(multiply_w1, now - 1)
-            at(take_max, now - 8)
-            at(multiply_w2, now - 7)
+            at(take_root, now - 3)
+            if now == 0:
+                spread_b1()
+                group_words(nc.vector.tensor_copy, w1_grouped, w1_raw)
             at(add_b1, now - 2)
-            at(deviation, now - 3)
+            at(take_max, now - 8)
+            at(negate_mean, now - 2)
+            at(transpose_z, now - 5)
             at(scale_relu, now - 5)
             at(group_r, now - 6)
-            if now == FIRST_PRODUCT:
-                spread_vectors()
-                w2_codes, w2_scales = quantise_weight(nc, const, w2_raw, G, "w2")
+            at(quantise_x, now)
+            if now == 0:
+                quantise(nc, w1_codes, w1_scales, w1_grouped)
+            at(quantise_r, now - 6)
+            at(transpose_x, now + 1)
+            at(multiply_w2, now - 7)
+            if now == 1:
+                group_words(nc.scalar.copy, w2_grouped, w2_raw)
+                turn_vectors()
+            if now == 2:
+                quantise(nc, w2_codes, w2_scales, w2_grouped)
 
         outT = psum_x.tile([P, G_CHUNKS, P], F32, tag="xT")
         for c in range(G_CHUNKS):

from contextlib import ExitStack

import concourse.masks as masks
import concourse.mybir as mybir

F32 = mybir.dt.float32
BF16 = mybir.dt.bfloat16
U32 = mybir.dt.uint32
U8 = mybir.dt.uint8
FP8X4 = mybir.dt.float8_e4m3fn_x4
ALU = mybir.AluOpType
ACT = mybir.ActivationFunctionType
AXIS = mybir.AxisListType

P = 128
PACK = 4
POLYLINES = 64
NODES = 64
H = 512
G = 256
EPS = 1e-5
TOKENS = POLYLINES * NODES
TILES = 2
UNIT = TILES * P
UNITS = TOKENS // UNIT
H_CHUNKS = H // P
G_CHUNKS = G // P
LINES_PER_UNIT = UNIT // NODES
WORDS = H // 2
LAST_LAG = 8
RUN = 4

FLOPS = 2 * TOKENS * H * H + 2 * TOKENS * H * G


def group_words(copy, grouped, planes):
    copy(
        out=grouped[:].rearrange("p (c i) t -> p c t i", i=RUN),
        in_=planes[:].rearrange("p t (c i) -> p c t i", i=RUN),
    )


def quantise(nc, codes, scales, grouped):
    nc.vector.quantize_mx(
        out=codes[:].bitcast(FP8X4),
        scales=scales[:],
        in_=grouped[:].rearrange("p c t -> p (c t)"),
    )


def tile_sub_graph_pb_kernel(tc, x_nodes, w1, b1, gamma, beta, w2, b2, out):
    nc = tc.nc
    x_flat = x_nodes.rearrange("b l k -> (b l) k")

    with ExitStack() as ctx:
        ctx.enter_context(tc.manual_schedule())
        const = ctx.enter_context(tc.tile_pool(name="const", bufs=1))
        x_pool = ctx.enter_context(tc.tile_pool(name="x", bufs=UNITS))
        two = ctx.enter_context(tc.tile_pool(name="two", bufs=2))
        three = ctx.enter_context(tc.tile_pool(name="three", bufs=3))
        psum_x = ctx.enter_context(tc.psum_pool(name="psum_x", bufs=1))
        psum_h = ctx.enter_context(tc.psum_pool(name="psum_h", bufs=2 * TILES))
        psum_z = ctx.enter_context(tc.psum_pool(name="psum_z", bufs=2))
        psum_x1 = ctx.enter_context(tc.psum_pool(name="psum_x1", bufs=1))

        x_sb = {}

        def load_x(unit):
            x_sb[unit] = x_pool.tile([P, TILES * H], BF16, name="x_sb")
            nc.sync.dma_start(
                out=x_sb[unit][:].rearrange("p (i k) -> p i k", i=TILES),
                in_=x_flat[unit * UNIT : (unit + 1) * UNIT, :].rearrange("(i p) k -> p i k", p=P),
            )

        load_x(0)
        w1_raw = const.tile([P, PACK, H], BF16)
        for u in range(2):
            nc.scalar.dma_start(
                out=w1_raw[:, 2 * u : 2 * u + 2, :],
                in_=w1[256 * u : 256 * u + 256, :].rearrange("(q e) c -> q e c", e=2),
            )
        load_x(1)
        b1_row = const.tile([P, H], BF16)
        nc.vector.memset(b1_row[:], 0.0)
        nc.scalar.dma_start(out=b1_row[0:1, :], in_=b1.rearrange("(o c) -> o c", o=1))
        rows_bf = const.tile([P, P], BF16)
        nc.vector.memset(rows_bf[:], 0.0)
        nc.scalar.dma_start(out=rows_bf[0:4, :], in_=gamma.rearrange("(t p) -> t p", p=P))
        nc.scalar.dma_start(out=rows_bf[4:8, :], in_=beta.rearrange("(t p) -> t p", p=P))
        nc.scalar.dma_start(out=rows_bf[8:10, :], in_=b2.rearrange("(t p) -> t p", p=P))
        eps_col = const.tile([P, 1], F32)
        nc.vector.memset(eps_col[:], EPS)
        warm = const.tile([P, 1], F32)
        nc.scalar.activation(out=warm[:], in_=eps_col[:], func=ACT.Sqrt)
        w2_raw = const.tile([P, PACK, G], BF16)
        nc.scalar.dma_start(out=w2_raw[:], in_=w2.rearrange("(t p) c -> p t c", p=P))
        for unit in range(2, UNITS):
            load_x(unit)

        ident = const.tile([P, P], F32)
        masks.make_identity(nc, ident[:])
        ones = const.tile([P, P], BF16)
        nc.vector.memset(ones[:], 1.0)
        best = const.tile([P, G_CHUNKS, P], F32)
        nc.vector.memset(best[:], 0.0)
        b1_all = const.tile([P, H], F32)
        cols = const.tile([P, 16], F32)

        w1_grouped = const.tile([P, H, PACK], BF16, align_bytes=64)
        w1_codes = const.tile([P, H], U32, align_bytes=64)
        w1_scales = const.tile([P, H], U8, align_bytes=64)
        w2_grouped = const.tile([P, G, PACK], BF16, align_bytes=64)
        w2_codes = const.tile([P, G], U32, align_bytes=64)
        w2_scales = const.tile([P, G], U8, align_bytes=64)

        def spread_b1():
            b1_ps = psum_z.tile([P, H], F32, tag="zT")
            nc.tensor.matmul(out=b1_ps[:], lhsT=ones[:], rhs=b1_row[:], start=True, stop=True)
            nc.scalar.copy(out=b1_all[:], in_=b1_ps[:])

        def turn_vectors():
            rows_f32 = const.tile([P, P], F32)
            nc.scalar.copy(out=rows_f32[:], in_=rows_bf[:])
            cols_ps = psum_z.tile([P, P], F32, tag="zT")
            nc.tensor.transpose(out=cols_ps[:], in_=rows_f32[:], identity=ident[:])
            nc.scalar.copy(out=cols[:], in_=cols_ps[:, 0:16])

        kept = {}

        def transpose_x(unit):
            x_words = x_sb[unit][:].bitcast(F32)
            xT = psum_x.tile([P, 2, UNIT], F32, tag="xT")
            for i in range(TILES):
                for u in range(2):
                    nc.tensor.transpose(
                        out=xT[:, u, i * P : (i + 1) * P],
                        in_=x_words[:, WORDS * i + P * u : WORDS * i + P * (u + 1)],
                        identity=ident[:],
                    )
            kept["xT", unit] = xT

        def group_x(unit):
            x_grouped = two.tile([P, UNIT, PACK], BF16, align_bytes=64)
            nc.scalar.copy(
                out=x_grouped[:].rearrange("p c t -> p (c t)").bitcast(F32).rearrange("p (c u) -> p c u", u=2),
                in_=kept["xT", unit][:].rearrange("p u c -> p c u"),
            )
            kept["x_grouped", unit] = x_grouped

        def quantise_x(unit):
            x_codes = two.tile([P, UNIT], U32, align_bytes=64)
            x_scales = two.tile([P, UNIT], U8, align_bytes=64)
            quantise(nc, x_codes, x_scales, kept["x_grouped", unit])
            kept["x_codes", unit] = x_codes
            kept["x_scales", unit] = x_scales

        def multiply_w1(unit):
            for i in range(TILES):
                h_ps = psum_h.tile([P, H], F32, tag="h_ps")
                nc.tensor.matmul_mx(
                    out=h_ps[:],
                    lhsT=kept["x_codes", unit][:, i * P : (i + 1) * P].bitcast(FP8X4),
                    lhsT_scale=kept["x_scales", unit][:, i * P : (i + 1) * P],
                    rhs=w1_codes[:].bitcast(FP8X4),
                    rhs_scale=w1_scales[:],
                    start=True,
                    stop=True,
                )
                kept["h_ps", unit, i] = h_ps

        def add_b1(unit):
            h = three.tile([P, TILES, H], F32)
            h_sum = two.tile([P, TILES], F32)
            for i in range(TILES):
                nc.vector.scalar_tensor_tensor(
                    out=h[:, i, :],
                    in0=kept["h_ps", unit, i][:],
                    scalar=1.0,
                    in1=b1_all[:],
                    op0=ALU.mult,
                    op1=ALU.add,
                    accum_out=h_sum[:, i : i + 1],
                )
            kept["h", unit] = h
            kept["h_sum", unit] = h_sum

        def negate_mean(unit):
            neg_mean = three.tile([P, TILES], F32)
            nc.vector.tensor_scalar_mul(out=neg_mean[:], in0=kept["h_sum", unit][:], scalar1=-1.0 / H)
            kept["neg_mean", unit] = neg_mean

        def sum_squares(unit):
            sq_sum = two.tile([P, TILES], F32)
            for i in range(TILES):
                squares = two.tile([P, H], BF16)
                nc.scalar.activation(
                    out=squares[:],
                    in_=kept["h", unit][:, i, :],
                    func=ACT.Square,
                    bias=kept["neg_mean", unit][:, i : i + 1],
                    accum_out=sq_sum[:, i : i + 1],
                )
            kept["sq_sum", unit] = sq_sum

        def take_root(unit):
            std = two.tile([P, TILES], F32)
            nc.scalar.activation(
                out=std[:], in_=kept["sq_sum", unit][:], func=ACT.Sqrt, bias=eps_col[:], scale=1.0 / H
            )
            kept["std", unit] = std

        def invert_std(unit):
            inv_std = two.tile([P, TILES], F32)
            nc.vector.reciprocal(out=inv_std[:], in_=kept["std", unit][:])
            kept["inv_std", unit] = inv_std

        def normalise(unit):
            z = two.tile([P, TILES, H], F32)
            for i in range(TILES):
                nc.gpsimd.tensor_scalar(
                    out=z[:, i, :],
                    in0=kept["h", unit][:, i, :],
                    scalar1=kept["neg_mean", unit][:, i : i + 1],
                    scalar2=kept["inv_std", unit][:, i : i + 1],
                    op0=ALU.add,
                    op1=ALU.mult,
                )
            kept["z", unit] = z

        def transpose_z(unit):
            for bank in range(2):
                zT = psum_z.tile([P, 2, UNIT], F32, tag="zT")
                for s in range(2):
                    t = 2 * bank + s
                    for i in range(TILES):
                        nc.tensor.transpose(
                            out=zT[:, s, i * P : (i + 1) * P],
                            in_=kept["z", unit][:, i, t * P : (t + 1) * P],
                            identity=ident[:],
                        )
                kept["zT", unit, bank] = zT

        def scale_relu(unit):
            r_planes = two.tile([P, H_CHUNKS, UNIT], BF16)
            for t in range(H_CHUNKS):
                nc.scalar.activation(
                    out=r_planes[:, t, :],
                    in_=kept["zT", unit, t // 2][:, t % 2, :],
                    func=ACT.Relu,
                    bias=cols[:, 4 + t : 5 + t],
                    scale=cols[:, t : t + 1],
                )
            kept["r_planes", unit] = r_planes

        def group_r(unit):
            r_grouped = two.tile([P, UNIT, PACK], BF16, align_bytes=64)
            group_words(nc.vector.tensor_copy, r_grouped, kept["r_planes", unit])
            kept["r_grouped", unit] = r_grouped

        def quantise_r(unit):
            r_codes = two.tile([P, UNIT], U32, align_bytes=64)
            r_scales = two.tile([P, UNIT], U8, align_bytes=64)
            quantise(nc, r_codes, r_scales, kept["r_grouped", unit])
            kept["r_codes", unit] = r_codes
            kept["r_scales", unit] = r_scales

        def multiply_w2(unit):
            x1_ps = psum_x1.tile([P, G_CHUNKS, UNIT], F32, tag="x1_ps")
            for c in range(G_CHUNKS):
                nc.tensor.matmul_mx(
                    out=x1_ps[:, c, :],
                    lhsT=w2_codes[:, c * P : (c + 1) * P].bitcast(FP8X4),
                    lhsT_scale=w2_scales[:, c * P : (c + 1) * P],
                    rhs=kept["r_codes", unit][:].bitcast(FP8X4),
                    rhs_scale=kept["r_scales", unit][:],
                    start=True,
                    stop=True,
                )
            kept["x1_ps", unit] = x1_ps

        def take_max(unit):
            nc.vector.tensor_reduce(
                out=best[:, :, unit * LINES_PER_UNIT : (unit + 1) * LINES_PER_UNIT],
                in_=kept["x1_ps", unit][:].rearrange("m c (b l) -> m c b l", l=NODES),
                axis=AXIS.X,
                op=ALU.max,
            )

        def at(step, unit):
            if 0 <= unit < UNITS:
                step(unit)

        transpose_x(0)
        for now in range(UNITS + LAST_LAG):
            at(multiply_w1, now - 1)
            at(invert_std, now - 4)
            at(normalise, now - 4)
            at(sum_squares, now - 3)
            at(group_x, now)
            at(take_root, now - 3)
            if now == 0:
                spread_b1()
                group_words(nc.vector.tensor_copy, w1_grouped, w1_raw)
            at(add_b1, now - 2)
            at(take_max, now - 8)
            at(negate_mean, now - 2)
            at(transpose_z, now - 5)
            at(scale_relu, now - 5)
            at(group_r, now - 6)
            at(quantise_x, now)
            if now == 0:
                quantise(nc, w1_codes, w1_scales, w1_grouped)
            at(quantise_r, now - 6)
            at(transpose_x, now + 1)
            at(multiply_w2, now - 7)
            if now == 1:
                group_words(nc.scalar.copy, w2_grouped, w2_raw)
                turn_vectors()
            if now == 2:
                quantise(nc, w2_codes, w2_scales, w2_grouped)

        outT = psum_x.tile([P, G_CHUNKS, P], F32, tag="xT")
        for c in range(G_CHUNKS):
            nc.vector.tensor_scalar_add(
                out=best[:, c, 0:POLYLINES], in0=best[:, c, 0:POLYLINES], scalar1=cols[:, 8 + c : 9 + c]
            )
            nc.tensor.transpose(out=outT[:, c, :], in_=best[:, c, :], identity=ident[:])
        out_sb = const.tile([P, G], F32)
        nc.vector.tensor_copy(out=out_sb[:], in_=outT[:].rearrange("b c m -> b (c m)"))
        nc.sync.dma_start(out=out[:, 0:G], in_=out_sb[0:POLYLINES, :])
        nc.sync.dma_start(out=out[:, G : 2 * G], in_=out_sb[0:POLYLINES, :])
